import numpy as np
import ml_dtypes


def mxq(x, axis, fmt="e4m3"):
    dtype, down = {"e4m3": (ml_dtypes.float8_e4m3fn, 7), "e5m2": (ml_dtypes.float8_e5m2, 14)}[fmt]
    v = np.moveaxis(np.asarray(x, np.float32).astype(ml_dtypes.bfloat16).astype(np.float64), axis, -1)
    blocks = v.reshape(v.shape[:-1] + (-1, 32))
    amax = np.abs(blocks).max(-1, keepdims=True)
    byte = np.maximum(np.where(amax > 0, np.frexp(amax)[1] - 1 + 127, 0) - down, 1)
    scale = np.exp2(byte - 127.0)
    codes = (blocks / scale).astype(np.float32).astype(dtype).astype(np.float64)
    return np.moveaxis((codes * scale).reshape(v.shape), -1, axis)


WIDE = False


def mx_kscale(k):
    if not WIDE:
        return np.ones(k)
    levels = np.array([10, -10, 5, -5, 0])
    a = np.random.permutation(np.resize(levels, k // 512 * 4)).reshape(k // 512, 4)
    idx = np.arange(k)
    return np.exp2(a[idx // 512, idx % 128 // 32])


BF16 = ml_dtypes.bfloat16


def bf(x):
    return np.asarray(x, np.float32).astype(BF16)


def f64(x):
    return np.asarray(x).astype(np.float64)


B, C, H, W, DM, GH = 6, 512, 32, 32, 128, 512


def sigmoid(v):
    return 1.0 / (1.0 + np.exp(-v))


def setup_inputs():
    s = np.concatenate([mx_kscale(C), np.ones(C)])
    t = mx_kscale(GH)
    return {'x': bf(np.random.standard_normal((B, C, H, W)) * s[:C][None, :, None, None]),
            'agg': bf(np.random.standard_normal((B, C, H, W)) * 0.7),
            'g1w': bf(np.random.standard_normal((GH, 2 * C)) / np.sqrt(2 * C) * t[:, None] / s[None, :]),
            'g1b': bf(np.random.standard_normal(GH) * 0.3 * t),
            'g2w': bf(np.random.standard_normal((C, GH)) * 2.0 / np.sqrt(GH) / t[None, :]),
            'g2b': bf(np.random.standard_normal(C) * 0.3)}


def reference(x, agg, g1w, g1b, g2w, g2b):
    a = f64(agg).reshape(B, C, H * W)
    cat = np.concatenate([f64(x).reshape(B, C, H * W), a], axis=1)
    hidden = np.maximum((mxq(f64(g1w), 1, 'e4m3') @ mxq(cat, 1, 'e4m3')) + f64(g1b)[None, :, None], 0.0)
    gate = sigmoid((mxq(f64(g2w), 1, 'e4m3') @ mxq(hidden, 1, 'e4m3')) + f64(g2b)[None, :, None])
    return (a * gate).reshape(B, C, H, W)

@@ -1,0 +1,266 @@
+from contextlib import ExitStack
+
+import concourse.mybir as mybir
+from concourse.masks import make_identity
+
+BF16 = mybir.dt.bfloat16
+F32 = mybir.dt.float32
+U32 = mybir.dt.uint32
+U8 = mybir.dt.uint8
+FP8X4 = mybir.dt.float8_e4m3fn_x4
+ACT = mybir.ActivationFunctionType
+ALU = mybir.AluOpType
+
+P = 128
+PACK = 4
+K_PASS = P * PACK
+
+IMAGES = 6
+CHANNELS = 512
+PIXELS = 1024
+STREAMS = 2
+UNIT = 512
+UNITS_PER_IMAGE = PIXELS // UNIT
+UNITS = IMAGES * UNITS_PER_IMAGE
+
+SCALAR_PIXELS = 224
+
+FLOPS = 2 * IMAGES * PIXELS * (CHANNELS * STREAMS * CHANNELS + CHANNELS * CHANNELS)
+
+
+def regroup(copy, grouped, slots):
+    copy(
+        out=grouped.rearrange("p (c i) j -> p c j i", i=4),
+        in_=slots.rearrange("p j (c i) -> p c j i", i=4),
+    )
+
+
+def tile_graphaugmentation_pb_t_kernel(tc, x, agg, g1w, g1b, g2w, g2b, out):
+    nc = tc.nc
+    x_view = x.rearrange("b (p j) h w -> b p j (h w)", j=PACK)
+    agg_view = agg.rearrange("b (p j) h w -> b p j (h w)", j=PACK)
+    out_view = out.rearrange("b (p j) h w -> b p j (h w)", j=PACK)
+
+    with ExitStack() as ctx:
+        keep = ctx.enter_context(tc.tile_pool(name="keep", bufs=1))
+        inputs = ctx.enter_context(tc.tile_pool(name="inputs", bufs=IMAGES))
+        work = ctx.enter_context(tc.tile_pool(name="work", bufs=2))
+        psum = ctx.enter_context(tc.psum_pool(name="psum", bufs=8))
+        ctx.enter_context(tc.manual_schedule())
+
+        w1_rows = keep.tile([P, PACK * STREAMS * K_PASS], BF16)
+        nc.sync.dma_start(out=w1_rows[:], in_=g1w.rearrange("(m j) k -> m (j k)", j=PACK))
+        w2_rows = keep.tile([P, PACK * K_PASS], BF16)
+        x_slots = []
+        agg_slots = []
+        for b in range(IMAGES):
+            x_image = inputs.tile([P, PACK, PIXELS], BF16, tag="x")
+            nc.sync.dma_start(out=x_image[:], in_=x_view[b])
+            x_slots.append(x_image)
+            agg_image = inputs.tile([P, PACK, PIXELS], BF16, tag="agg")
+            nc.sync.dma_start(out=agg_image[:], in_=agg_view[b])
+            agg_slots.append(agg_image)
+            if b == 0:
+                nc.sync.dma_start(
+                    out=w2_rows[:], in_=g2w.rearrange("(m j) k -> m (j k)", j=PACK)
+                )
+
+        table_warmer = keep.tile([P, 1], F32)
+        nc.vector.memset(table_warmer[:], 0.0)
+        nc.scalar.activation(out=table_warmer[:], in_=table_warmer[:], func=ACT.Sigmoid)
+
+        bias1_bf16 = keep.tile([P, PACK], BF16)
+        nc.scalar.dma_start(out=bias1_bf16[:], in_=g1b.rearrange("(m j) -> m j", j=PACK))
+        bias2_bf16 = keep.tile([P, PACK], BF16)
+        nc.scalar.dma_start(out=bias2_bf16[:], in_=g2b.rearrange("(m j) -> m j", j=PACK))
+        bias1 = keep.tile([P, PACK], F32)
+        nc.vector.tensor_copy(out=bias1[:], in_=bias1_bf16[:])
+        bias2 = keep.tile([P, PACK], F32)
+        nc.vector.tensor_copy(out=bias2[:], in_=bias2_bf16[:])
+
+        identity = keep.tile([P, P], F32)
+        make_identity(nc, identity[:])
+
+        def transpose_weight(rows, passes, grouped):
+            tiles = PACK * passes
+            words = rows[:].bitcast(F32).rearrange("m (c p u) -> m c u p", c=tiles, u=2)
+            grouped_words = grouped[:].bitcast(F32).rearrange(
+                "p (c m u) -> p c m u", c=tiles, u=2
+            )
+            for pair in range(tiles // 2):
+                bank = psum.tile([P, UNIT], F32, tag="bank")
+                transposed = bank[:].rearrange("p (c u m) -> p c u m", c=2, u=2)
+                for c in range(2):
+                    for u in range(2):
+                        nc.tensor.transpose(
+                            transposed[:, c, u, :], words[:, 2 * pair + c, u, :], identity[:]
+                        )
+                copy = nc.vector.tensor_copy if pair % 2 == 0 else nc.scalar.copy
+                copy(
+                    out=grouped_words[:, 2 * pair : 2 * pair + 2, :, :],
+                    in_=transposed.rearrange("p c u m -> p c m u"),
+                )
+
+        def quantise_weight(grouped, codes, scales):
+            nc.vector.quantize_mx(
+                out=codes[:].bitcast(FP8X4), scales=scales[:], in_=grouped[:]
+            )
+
+        w1_grouped = keep.tile([P, PACK * STREAMS * P * PACK], BF16, align_bytes=64)
+        w1_codes = keep.tile([P, PACK * STREAMS * P], U32, align_bytes=64)
+        w1_scales = keep.tile([P, PACK * STREAMS * P], U8, align_bytes=64)
+        w2_grouped = keep.tile([P, PACK * P * PACK], BF16, align_bytes=64)
+        w2_codes = keep.tile([P, PACK * P], U32, align_bytes=64)
+        w2_scales = keep.tile([P, PACK * P], U8, align_bytes=64)
+
+        cat_grouped = {}
+        cat_codes = {}
+        cat_scales = {}
+        hidden_banks = {}
+        hidden_slots = {}
+        hidden_grouped = {}
+        hidden_codes = {}
+        hidden_scales = {}
+        gate_banks = {}
+        gate_slots = {}
+
+        def pixels_of(unit):
+            image, half = divmod(unit, UNITS_PER_IMAGE)
+            return image, half * UNIT
+
+        def regroup_cat(unit):
+            image, first = pixels_of(unit)
+            border = first + SCALAR_PIXELS
+            grouped = work.tile(
+                [P, STREAMS, UNIT, PACK], BF16, tag="cat_grouped", bufs=3, align_bytes=64
+            )
+            for s, slots in enumerate((x_slots[image], agg_slots[image])):
+                regroup(
+                    nc.scalar.copy,
+                    grouped[:, s, :SCALAR_PIXELS, :],
+                    slots[:, :, first:border],
+                )
+                regroup(
+                    nc.vector.tensor_copy,
+                    grouped[:, s, SCALAR_PIXELS:, :],
+                    slots[:, :, border : first + UNIT],
+                )
+            cat_grouped[unit] = grouped
+
+        def quantise_cat(unit):
+            codes = work.tile([P, STREAMS, UNIT], U32, tag="cat_codes", align_bytes=64)
+            scales = work.tile([P, STREAMS, UNIT], U8, tag="cat_scales", align_bytes=64)
+            nc.vector.quantize_mx(
+                out=codes[:].rearrange("p s w -> p (s w)").bitcast(FP8X4),
+                scales=scales[:].rearrange("p s w -> p (s w)"),
+                in_=cat_grouped[unit][:].rearrange("p s w j -> p (s w j)"),
+            )
+            cat_codes[unit] = codes
+            cat_scales[unit] = scales
+
+        def first_matmul(unit):
+            for j in range(PACK):
+                bank = psum.tile([P, UNIT], F32, tag="bank")
+                for s in range(STREAMS):
+                    columns = slice((j * STREAMS + s) * P, (j * STREAMS + s + 1) * P)
+                    nc.tensor.matmul_mx(
+                        out=bank[:],
+                        lhsT=w1_codes[:, columns].bitcast(FP8X4),
+                        lhsT_scale=w1_scales[:, columns],
+                        rhs=cat_codes[unit][:, s, :].bitcast(FP8X4),
+                        rhs_scale=cat_scales[unit][:, s, :],
+                        start=(s == 0),
+                        stop=(s == STREAMS - 1),
+                    )
+                hidden_banks[unit, j] = bank
+
+        def relu_hidden(unit):
+            slots = work.tile([P, PACK, UNIT], BF16, tag="hidden_slots")
+            for j in range(PACK):
+                nc.scalar.activation(
+                    out=slots[:, j, :],
+                    in_=hidden_banks[unit, j][:],
+                    func=ACT.Relu,
+                    bias=bias1[:, j : j + 1],
+                )
+            hidden_slots[unit] = slots
+
+        def regroup_hidden(unit):
+            grouped = work.tile([P, UNIT, PACK], BF16, tag="hidden_grouped", align_bytes=64)
+            regroup(nc.vector.tensor_copy, grouped[:], hidden_slots[unit][:])
+            hidden_grouped[unit] = grouped
+
+        def quantise_hidden(unit):
+            codes = work.tile([P, UNIT], U32, tag="hidden_codes", align_bytes=64)
+            scales = work.tile([P, UNIT], U8, tag="hidden_scales", align_bytes=64)
+            nc.vector.quantize_mx(
+                out=codes[:].bitcast(FP8X4),
+                scales=scales[:],
+                in_=hidden_grouped[unit][:].rearrange("p w j -> p (w j)"),
+            )
+            hidden_codes[unit] = codes
+            hidden_scales[unit] = scales
+
+        def second_matmul(unit):
+            for j in range(PACK):
+                bank = psum.tile([P, UNIT], F32, tag="bank")
+                columns = slice(j * P, (j + 1) * P)
+                nc.tensor.matmul_mx(
+                    out=bank[:],
+                    lhsT=w2_codes[:, columns].bitcast(FP8X4),
+                    lhsT_scale=w2_scales[:, columns],
+                    rhs=hidden_codes[unit][:].bitcast(FP8X4),
+                    rhs_scale=hidden_scales[unit][:],
+                    start=True,
+                    stop=True,
+                )
+                gate_banks[unit, j] = bank
+
+        def sigmoid_gate(unit):
+            slots = work.tile([P, PACK, UNIT], F32, tag="gate_slots", bufs=4)
+            for j in range(PACK):
+                nc.scalar.activation(
+                    out=slots[:, j, :],
+                    in_=gate_banks[unit, j][:],
+                    func=ACT.Sigmoid,
+                    bias=bias2[:, j : j + 1],
+                )
+            gate_slots[unit] = slots
+
+        def multiply_and_store(unit):
+            image, first = pixels_of(unit)
+            result = gate_slots[unit]
+            nc.vector.tensor_tensor(
+                out=result[:],
+                in0=result[:],
+                in1=agg_slots[image][:, :, first : first + UNIT],
+                op=ALU.mult,
+            )
+            nc.sync.dma_start(out=out_view[image][:, :, first : first + UNIT], in_=result[:])
+
+        transpose_weight(w1_rows, STREAMS, w1_grouped)
+        regroup_cat(0)
+        quantise_weight(w1_grouped, w1_codes, w1_scales)
+        quantise_cat(0)
+        first_matmul(0)
+        transpose_weight(w2_rows, 1, w2_grouped)
+        regroup_cat(1)
+        quantise_weight(w2_grouped, w2_codes, w2_scales)
+
+        for i in range(UNITS + 2):
+            if i < UNITS:
+                relu_hidden(i)
+            if i >= 2:
+                multiply_and_store(i - 2)
+            if i < UNITS:
+                regroup_hidden(i)
+            if 1 <= i <= UNITS:
+                sigmoid_gate(i - 1)
+            if i + 1 < UNITS:
+                quantise_cat(i + 1)
+                first_matmul(i + 1)
+            if i < UNITS:
+                quantise_hidden(i)
+                second_matmul(i)
+            if i + 2 < UNITS:
+                regroup_cat(i + 2)

@@ -48,22 +48,29 @@ def tile_graphaugmentation_pb_t_kernel(tc, x, agg, g1w, g1b, g2w, g2b, out):
         psum = ctx.enter_context(tc.psum_pool(name="psum", bufs=8))
         ctx.enter_context(tc.manual_schedule())
 
-        w1_rows = keep.tile([P, PACK * STREAMS * K_PASS], BF16)
-        nc.sync.dma_start(out=w1_rows[:], in_=g1w.rearrange("(m j) k -> m (j k)", j=PACK))
-        w2_rows = keep.tile([P, PACK * K_PASS], BF16)
         x_slots = []
         agg_slots = []
         for b in range(IMAGES):
             x_image = inputs.tile([P, PACK, PIXELS], BF16, tag="x")
-            nc.sync.dma_start(out=x_image[:], in_=x_view[b])
             x_slots.append(x_image)
             agg_image = inputs.tile([P, PACK, PIXELS], BF16, tag="agg")
-            nc.sync.dma_start(out=agg_image[:], in_=agg_view[b])
             agg_slots.append(agg_image)
-            if b == 0:
-                nc.sync.dma_start(
-                    out=w2_rows[:], in_=g2w.rearrange("(m j) k -> m (j k)", j=PACK)
-                )
+
+        def load_pixels(image, first, count):
+            columns = slice(first, first + count)
+            nc.sync.dma_start(out=x_slots[image][:, :, columns], in_=x_view[image][:, :, columns])
+            nc.sync.dma_start(
+                out=agg_slots[image][:, :, columns], in_=agg_view[image][:, :, columns]
+            )
+
+        w1_rows = keep.tile([P, PACK * STREAMS * K_PASS], BF16)
+        nc.sync.dma_start(out=w1_rows[:], in_=g1w.rearrange("(m j) k -> m (j k)", j=PACK))
+        load_pixels(0, 0, UNIT)
+        w2_rows = keep.tile([P, PACK * K_PASS], BF16)
+        nc.sync.dma_start(out=w2_rows[:], in_=g2w.rearrange("(m j) k -> m (j k)", j=PACK))
+        load_pixels(0, UNIT, UNIT)
+        for b in range(1, IMAGES):
+            load_pixels(b, 0, PIXELS)
 
         table_warmer = keep.tile([P, 1], F32)
         nc.vector.memset(table_warmer[:], 0.0)
@@ -227,40 +234,46 @@ def tile_graphaugmentation_pb_t_kernel(tc, x, agg, g1w, g1b, g2w, g2b, out):
                 )
             gate_slots[unit] = slots
 
-        def multiply_and_store(unit):
+        def multiply_and_store(unit, pieces):
             image, first = pixels_of(unit)
+            columns = slice(first, first + UNIT)
             result = gate_slots[unit]
-            nc.vector.tensor_tensor(
-                out=result[:],
-                in0=result[:],
-                in1=agg_slots[image][:, :, first : first + UNIT],
-                op=ALU.mult,
-            )
-            nc.sync.dma_start(out=out_view[image][:, :, first : first + UNIT], in_=result[:])
+            for piece in range(pieces):
+                slots = slice(piece * PACK // pieces, (piece + 1) * PACK // pieces)
+                nc.vector.tensor_tensor(
+                    out=result[:, slots, :],
+                    in0=result[:, slots, :],
+                    in1=agg_slots[image][:, slots, columns],
+                    op=ALU.mult,
+                )
+                nc.sync.dma_start(
+                    out=out_view[image][:, slots, columns], in_=result[:, slots, :]
+                )
 
         transpose_weight(w1_rows, STREAMS, w1_grouped)
         regroup_cat(0)
+        transpose_weight(w2_rows, 1, w2_grouped)
         quantise_weight(w1_grouped, w1_codes, w1_scales)
         quantise_cat(0)
         first_matmul(0)
-        transpose_weight(w2_rows, 1, w2_grouped)
         regroup_cat(1)
         quantise_weight(w2_grouped, w2_codes, w2_scales)
 
         for i in range(UNITS + 2):
-            if i < UNITS:
-                relu_hidden(i)
-            if i >= 2:
-                multiply_and_store(i - 2)
-            if i < UNITS:
-                regroup_hidden(i)
-            if 1 <= i <= UNITS:
-                sigmoid_gate(i - 1)
             if i + 1 < UNITS:
                 quantise_cat(i + 1)
+            if i < UNITS:
+                relu_hidden(i)
+            if i + 1 < UNITS:
                 first_matmul(i + 1)
+            if i >= 2:
+                multiply_and_store(i - 2, pieces=PACK if i - 2 == UNITS - 1 else 1)
+            if i < UNITS:
+                regroup_hidden(i)
+            if i + 2 < UNITS:
+                regroup_cat(i + 2)
+            if 1 <= i <= UNITS:
+                sigmoid_gate(i - 1)
             if i < UNITS:
                 quantise_hidden(i)
                 second_matmul(i)
-            if i + 2 < UNITS:
-                regroup_cat(i + 2)

@@ -23,7 +23,8 @@ UNIT = 512
 UNITS_PER_IMAGE = PIXELS // UNIT
 UNITS = IMAGES * UNITS_PER_IMAGE
 
-SCALAR_PIXELS = 224
+SCALAR_PIXELS = 192
+GPSIMD_PIXELS = 160
 
 FLOPS = 2 * IMAGES * PIXELS * (CHANNELS * STREAMS * CHANNELS + CHANNELS * CHANNELS)
 
@@ -37,31 +38,34 @@ def regroup(copy, grouped, slots):
 
 def tile_graphaugmentation_pb_t_kernel(tc, x, agg, g1w, g1b, g2w, g2b, out):
     nc = tc.nc
-    x_view = x.rearrange("b (p j) h w -> b p j (h w)", j=PACK)
-    agg_view = agg.rearrange("b (p j) h w -> b p j (h w)", j=PACK)
+    stream_views = [
+        x.rearrange("b (p j) h w -> b p j (h w)", j=PACK),
+        agg.rearrange("b (p j) h w -> b p j (h w)", j=PACK),
+    ]
     out_view = out.rearrange("b (p j) h w -> b p j (h w)", j=PACK)
 
     with ExitStack() as ctx:
         keep = ctx.enter_context(tc.tile_pool(name="keep", bufs=1))
         inputs = ctx.enter_context(tc.tile_pool(name="inputs", bufs=IMAGES))
         work = ctx.enter_context(tc.tile_pool(name="work", bufs=2))
-        psum = ctx.enter_context(tc.psum_pool(name="psum", bufs=8))
+        scalar_banks = ctx.enter_context(tc.psum_pool(name="scalar_banks", bufs=4))
+        vector_banks = ctx.enter_context(tc.psum_pool(name="vector_banks", bufs=4))
         ctx.enter_context(tc.manual_schedule())
 
-        x_slots = []
-        agg_slots = []
+        stream_slots = [[], []]
         for b in range(IMAGES):
             x_image = inputs.tile([P, PACK, PIXELS], BF16, tag="x")
-            x_slots.append(x_image)
+            stream_slots[0].append(x_image)
             agg_image = inputs.tile([P, PACK, PIXELS], BF16, tag="agg")
-            agg_slots.append(agg_image)
+            stream_slots[1].append(agg_image)
 
         def load_pixels(image, first, count):
             columns = slice(first, first + count)
-            nc.sync.dma_start(out=x_slots[image][:, :, columns], in_=x_view[image][:, :, columns])
-            nc.sync.dma_start(
-                out=agg_slots[image][:, :, columns], in_=agg_view[image][:, :, columns]
-            )
+            for s in range(STREAMS):
+                nc.sync.dma_start(
+                    out=stream_slots[s][image][:, :, columns],
+                    in_=stream_views[s][image][:, :, columns],
+                )
 
         w1_rows = keep.tile([P, PACK * STREAMS * K_PASS], BF16)
         nc.sync.dma_start(out=w1_rows[:], in_=g1w.rearrange("(m j) k -> m (j k)", j=PACK))
@@ -85,8 +89,10 @@ def tile_graphaugmentation_pb_t_kernel(tc, x, agg, g1w, g1b, g2w, g2b, out):
         bias2 = keep.tile([P, PACK], F32)
         nc.vector.tensor_copy(out=bias2[:], in_=bias2_bf16[:])
 
-        identity = keep.tile([P, P], F32)
-        make_identity(nc, identity[:])
+        identity_f32 = keep.tile([P, P], F32)
+        make_identity(nc, identity_f32[:])
+        identity_bf16 = keep.tile([P, P], BF16)
+        make_identity(nc, identity_bf16[:])
 
         def transpose_weight(rows, passes, grouped):
             tiles = PACK * passes
@@ -95,14 +101,20 @@ def tile_graphaugmentation_pb_t_kernel(tc, x, agg, g1w, g1b, g2w, g2b, out):
                 "p (c m u) -> p c m u", c=tiles, u=2
             )
             for pair in range(tiles // 2):
-                bank = psum.tile([P, UNIT], F32, tag="bank")
+                if pair % 2 == 0:
+                    bank = vector_banks.tile([P, UNIT], F32, tag="bank")
+                    copy = nc.vector.tensor_copy
+                else:
+                    bank = scalar_banks.tile([P, UNIT], F32, tag="bank")
+                    copy = nc.scalar.copy
                 transposed = bank[:].rearrange("p (c u m) -> p c u m", c=2, u=2)
                 for c in range(2):
                     for u in range(2):
                         nc.tensor.transpose(
-                            transposed[:, c, u, :], words[:, 2 * pair + c, u, :], identity[:]
+                            transposed[:, c, u, :],
+                            words[:, 2 * pair + c, u, :],
+                            identity_f32[:],
                         )
-                copy = nc.vector.tensor_copy if pair % 2 == 0 else nc.scalar.copy
                 copy(
                     out=grouped_words[:, 2 * pair : 2 * pair + 2, :, :],
                     in_=transposed.rearrange("p c u m -> p c m u"),
@@ -121,61 +133,65 @@ def tile_graphaugmentation_pb_t_kernel(tc, x, agg, g1w, g1b, g2w, g2b, out):
         w2_scales = keep.tile([P, PACK * P], U8, align_bytes=64)
 
         cat_grouped = {}
-        cat_codes = {}
-        cat_scales = {}
+        cat_quantised = {}
         hidden_banks = {}
         hidden_slots = {}
         hidden_grouped = {}
-        hidden_codes = {}
-        hidden_scales = {}
+        hidden_quantised = {}
         gate_banks = {}
         gate_slots = {}
+        agg_banks = {}
 
         def pixels_of(unit):
             image, half = divmod(unit, UNITS_PER_IMAGE)
-            return image, half * UNIT
+            return image, slice(half * UNIT, (half + 1) * UNIT)
 
-        def regroup_cat(unit):
-            image, first = pixels_of(unit)
-            border = first + SCALAR_PIXELS
+        def regroup_stream(unit, s):
+            image, columns = pixels_of(unit)
+            slots = stream_slots[s][image][:, :, columns]
             grouped = work.tile(
-                [P, STREAMS, UNIT, PACK], BF16, tag="cat_grouped", bufs=3, align_bytes=64
+                [P, UNIT, PACK], BF16, tag="cat_grouped", bufs=3 * STREAMS, align_bytes=64
             )
-            for s, slots in enumerate((x_slots[image], agg_slots[image])):
-                regroup(
-                    nc.scalar.copy,
-                    grouped[:, s, :SCALAR_PIXELS, :],
-                    slots[:, :, first:border],
-                )
-                regroup(
-                    nc.vector.tensor_copy,
-                    grouped[:, s, SCALAR_PIXELS:, :],
-                    slots[:, :, border : first + UNIT],
-                )
-            cat_grouped[unit] = grouped
+            scalar_end = SCALAR_PIXELS
+            gpsimd_end = SCALAR_PIXELS + GPSIMD_PIXELS
+            regroup(nc.scalar.copy, grouped[:, :scalar_end, :], slots[:, :, :scalar_end])
+            nc.gpsimd.tensor_scalar(
+                out=grouped[:, scalar_end:gpsimd_end, :],
+                in0=slots[:, :, scalar_end:gpsimd_end].rearrange("p j w -> p w j"),
+                scalar1=1.0,
+                scalar2=0.0,
+                op0=ALU.mult,
+                op1=ALU.add,
+            )
+            regroup(nc.vector.tensor_copy, grouped[:, gpsimd_end:, :], slots[:, :, gpsimd_end:])
+            cat_grouped[unit, s] = grouped
+
+        def quantise(grouped, tag, bufs):
+            codes = work.tile([P, UNIT], U32, tag=tag + "_codes", bufs=bufs, align_bytes=64)
+            scales = work.tile([P, UNIT], U8, tag=tag + "_scales", bufs=bufs, align_bytes=64)
+            nc.vector.quantize_mx(
+                out=codes[:].bitcast(FP8X4),
+                scales=scales[:],
+                in_=grouped[:].rearrange("p w j -> p (w j)"),
+            )
+            return codes, scales
 
         def quantise_cat(unit):
-            codes = work.tile([P, STREAMS, UNIT], U32, tag="cat_codes", align_bytes=64)
-            scales = work.tile([P, STREAMS, UNIT], U8, tag="cat_scales", align_bytes=64)
-            nc.vector.quantize_mx(
-                out=codes[:].rearrange("p s w -> p (s w)").bitcast(FP8X4),
-                scales=scales[:].rearrange("p s w -> p (s w)"),
-                in_=cat_grouped[unit][:].rearrange("p s w j -> p (s w j)"),
-            )
-            cat_codes[unit] = codes
-            cat_scales[unit] = scales
+            for s in range(STREAMS):
+                cat_quantised[unit, s] = quantise(cat_grouped[unit, s], "cat", 2 * STREAMS)
 
         def first_matmul(unit):
             for j in range(PACK):
-                bank = psum.tile([P, UNIT], F32, tag="bank")
+                bank = scalar_banks.tile([P, UNIT], F32, tag="bank")
                 for s in range(STREAMS):
                     columns = slice((j * STREAMS + s) * P, (j * STREAMS + s + 1) * P)
+                    codes, scales = cat_quantised[unit, s]
                     nc.tensor.matmul_mx(
                         out=bank[:],
                         lhsT=w1_codes[:, columns].bitcast(FP8X4),
                         lhsT_scale=w1_scales[:, columns],
-                        rhs=cat_codes[unit][:, s, :].bitcast(FP8X4),
-                        rhs_scale=cat_scales[unit][:, s, :],
+                        rhs=codes[:].bitcast(FP8X4),
+                        rhs_scale=scales[:],
                         start=(s == 0),
                         stop=(s == STREAMS - 1),
                     )
@@ -198,26 +214,19 @@ def tile_graphaugmentation_pb_t_kernel(tc, x, agg, g1w, g1b, g2w, g2b, out):
             hidden_grouped[unit] = grouped
 
         def quantise_hidden(unit):
-            codes = work.tile([P, UNIT], U32, tag="hidden_codes", align_bytes=64)
-            scales = work.tile([P, UNIT], U8, tag="hidden_scales", align_bytes=64)
-            nc.vector.quantize_mx(
-                out=codes[:].bitcast(FP8X4),
-                scales=scales[:],
-                in_=hidden_grouped[unit][:].rearrange("p w j -> p (w j)"),
-            )
-            hidden_codes[unit] = codes
-            hidden_scales[unit] = scales
+            hidden_quantised[unit] = quantise(hidden_grouped[unit], "hidden", 2)
 
         def second_matmul(unit):
+            codes, scales = hidden_quantised[unit]
             for j in range(PACK):
-                bank = psum.tile([P, UNIT], F32, tag="bank")
+                bank = scalar_banks.tile([P, UNIT], F32, tag="bank")
                 columns = slice(j * P, (j + 1) * P)
                 nc.tensor.matmul_mx(
                     out=bank[:],
                     lhsT=w2_codes[:, columns].bitcast(FP8X4),
                     lhsT_scale=w2_scales[:, columns],
-                    rhs=hidden_codes[unit][:].bitcast(FP8X4),
-                    rhs_scale=hidden_scales[unit][:],
+                    rhs=codes[:].bitcast(FP8X4),
+                    rhs_scale=scales[:],
                     start=True,
                     stop=True,
                 )
@@ -234,29 +243,44 @@ def tile_graphaugmentation_pb_t_kernel(tc, x, agg, g1w, g1b, g2w, g2b, out):
                 )
             gate_slots[unit] = slots
 
-        def multiply_and_store(unit, pieces):
-            image, first = pixels_of(unit)
-            columns = slice(first, first + UNIT)
+        def agg_to_psum(unit):
+            image, columns = pixels_of(unit)
+            for j in range(PACK):
+                bank = vector_banks.tile([P, UNIT], F32, tag="bank")
+                nc.tensor.matmul(
+                    out=bank[:],
+                    lhsT=identity_bf16[:],
+                    rhs=stream_slots[1][image][:, j, columns],
+                    start=True,
+                    stop=True,
+                )
+                agg_banks[unit, j] = bank
+
+        def multiply_and_store(unit, slots_in_a_store):
+            image, columns = pixels_of(unit)
             result = gate_slots[unit]
-            for piece in range(pieces):
-                slots = slice(piece * PACK // pieces, (piece + 1) * PACK // pieces)
+            for j in range(PACK):
                 nc.vector.tensor_tensor(
-                    out=result[:, slots, :],
-                    in0=result[:, slots, :],
-                    in1=agg_slots[image][:, slots, columns],
+                    out=result[:, j, :],
+                    in0=agg_banks[unit, j][:],
+                    in1=result[:, j, :],
                     op=ALU.mult,
                 )
-                nc.sync.dma_start(
-                    out=out_view[image][:, slots, columns], in_=result[:, slots, :]
-                )
+                if (j + 1) % slots_in_a_store == 0:
+                    done = slice(j + 1 - slots_in_a_store, j + 1)
+                    nc.sync.dma_start(
+                        out=out_view[image][:, done, columns], in_=result[:, done, :]
+                    )
 
         transpose_weight(w1_rows, STREAMS, w1_grouped)
-        regroup_cat(0)
+        regroup_stream(0, 0)
+        regroup_stream(0, 1)
         transpose_weight(w2_rows, 1, w2_grouped)
         quantise_weight(w1_grouped, w1_codes, w1_scales)
         quantise_cat(0)
         first_matmul(0)
-        regroup_cat(1)
+        regroup_stream(1, 0)
+        regroup_stream(1, 1)
         quantise_weight(w2_grouped, w2_codes, w2_scales)
 
         for i in range(UNITS + 2):
@@ -264,16 +288,21 @@ def tile_graphaugmentation_pb_t_kernel(tc, x, agg, g1w, g1b, g2w, g2b, out):
                 quantise_cat(i + 1)
             if i < UNITS:
                 relu_hidden(i)
-            if i + 1 < UNITS:
-                first_matmul(i + 1)
+            if 1 <= i <= UNITS:
+                second_matmul(i - 1)
             if i >= 2:
-                multiply_and_store(i - 2, pieces=PACK if i - 2 == UNITS - 1 else 1)
+                multiply_and_store(i - 2, slots_in_a_store=1 if i - 2 == UNITS - 1 else PACK)
+            if 1 <= i <= UNITS:
+                agg_to_psum(i - 1)
             if i < UNITS:
                 regroup_hidden(i)
             if i + 2 < UNITS:
-                regroup_cat(i + 2)
+                regroup_stream(i + 2, 0)
             if 1 <= i <= UNITS:
                 sigmoid_gate(i - 1)
+            if i + 1 < UNITS:
+                first_matmul(i + 1)
+            if i + 2 < UNITS:
+                regroup_stream(i + 2, 1)
             if i < UNITS:
                 quantise_hidden(i)
-                second_matmul(i)

@@ -24,7 +24,6 @@ UNITS_PER_IMAGE = PIXELS // UNIT
 UNITS = IMAGES * UNITS_PER_IMAGE
 
 SCALAR_PIXELS = 192
-GPSIMD_PIXELS = 160
 
 FLOPS = 2 * IMAGES * PIXELS * (CHANNELS * STREAMS * CHANNELS + CHANNELS * CHANNELS)
 
@@ -152,18 +151,24 @@ def tile_graphaugmentation_pb_t_kernel(tc, x, agg, g1w, g1b, g2w, g2b, out):
             grouped = work.tile(
                 [P, UNIT, PACK], BF16, tag="cat_grouped", bufs=3 * STREAMS, align_bytes=64
             )
-            scalar_end = SCALAR_PIXELS
-            gpsimd_end = SCALAR_PIXELS + GPSIMD_PIXELS
-            regroup(nc.scalar.copy, grouped[:, :scalar_end, :], slots[:, :, :scalar_end])
-            nc.gpsimd.tensor_scalar(
-                out=grouped[:, scalar_end:gpsimd_end, :],
-                in0=slots[:, :, scalar_end:gpsimd_end].rearrange("p j w -> p w j"),
-                scalar1=1.0,
-                scalar2=0.0,
-                op0=ALU.mult,
-                op1=ALU.add,
+            regroup(
+                nc.scalar.copy, grouped[:, :SCALAR_PIXELS, :], slots[:, :, :SCALAR_PIXELS]
             )
-            regroup(nc.vector.tensor_copy, grouped[:, gpsimd_end:, :], slots[:, :, gpsimd_end:])
+            if s == 0:
+                nc.gpsimd.tensor_scalar(
+                    out=grouped[:, SCALAR_PIXELS:, :],
+                    in0=slots[:, :, SCALAR_PIXELS:].rearrange("p j w -> p w j"),
+                    scalar1=1.0,
+                    scalar2=0.0,
+                    op0=ALU.mult,
+                    op1=ALU.add,
+                )
+            else:
+                regroup(
+                    nc.vector.tensor_copy,
+                    grouped[:, SCALAR_PIXELS:, :],
+                    slots[:, :, SCALAR_PIXELS:],
+                )
             cat_grouped[unit, s] = grouped
 
         def quantise(grouped, tag, bufs):

@@ -250,29 +250,32 @@ def tile_graphaugmentation_pb_t_kernel(tc, x, agg, g1w, g1b, g2w, g2b, out):
 
         def agg_to_psum(unit):
             image, columns = pixels_of(unit)
-            for j in range(PACK):
-                bank = vector_banks.tile([P, UNIT], F32, tag="bank")
-                nc.tensor.matmul(
-                    out=bank[:],
-                    lhsT=identity_bf16[:],
-                    rhs=stream_slots[1][image][:, j, columns],
-                    start=True,
-                    stop=True,
-                )
-                agg_banks[unit, j] = bank
+            for pair in range(PACK // 2):
+                bank = vector_banks.tile([P, 2, UNIT], BF16, tag="bank")
+                for e in range(2):
+                    nc.tensor.matmul(
+                        out=bank[:, e, :],
+                        lhsT=identity_bf16[:],
+                        rhs=stream_slots[1][image][:, 2 * pair + e, columns],
+                        start=True,
+                        stop=True,
+                    )
+                agg_banks[unit, pair] = bank
 
         def multiply_and_store(unit, slots_in_a_store):
             image, columns = pixels_of(unit)
             result = gate_slots[unit]
-            for j in range(PACK):
+            slots_in_a_product = min(2, slots_in_a_store)
+            for j in range(0, PACK, slots_in_a_product):
+                slots = slice(j, j + slots_in_a_product)
                 nc.vector.tensor_tensor(
-                    out=result[:, j, :],
-                    in0=agg_banks[unit, j][:],
-                    in1=result[:, j, :],
+                    out=result[:, slots, :],
+                    in0=agg_banks[unit, j // 2][:, j % 2 : j % 2 + slots_in_a_product, :],
+                    in1=result[:, slots, :],
                     op=ALU.mult,
                 )
-                if (j + 1) % slots_in_a_store == 0:
-                    done = slice(j + 1 - slots_in_a_store, j + 1)
+                if (j + slots_in_a_product) % slots_in_a_store == 0:
+                    done = slice(j + slots_in_a_product - slots_in_a_store, j + slots_in_a_product)
                     nc.sync.dma_start(
                         out=out_view[image][:, done, columns], in_=result[:, done, :]
                     )

@@ -47,8 +47,8 @@ def tile_graphaugmentation_pb_t_kernel(tc, x, agg, g1w, g1b, g2w, g2b, out):
         keep = ctx.enter_context(tc.tile_pool(name="keep", bufs=1))
         inputs = ctx.enter_context(tc.tile_pool(name="inputs", bufs=IMAGES))
         work = ctx.enter_context(tc.tile_pool(name="work", bufs=2))
-        scalar_banks = ctx.enter_context(tc.psum_pool(name="scalar_banks", bufs=4))
-        vector_banks = ctx.enter_context(tc.psum_pool(name="vector_banks", bufs=4))
+        scalar_banks = ctx.enter_context(tc.psum_pool(name="scalar_banks", bufs=6))
+        vector_banks = ctx.enter_context(tc.psum_pool(name="vector_banks", bufs=2))
         ctx.enter_context(tc.manual_schedule())
 
         stream_slots = [[], []]

@@ -25,6 +25,8 @@ UNITS = IMAGES * UNITS_PER_IMAGE
 
 SCALAR_PIXELS = 192
 
+FIRST_GPSIMD_UNIT = 5
+
 FLOPS = 2 * IMAGES * PIXELS * (CHANNELS * STREAMS * CHANNELS + CHANNELS * CHANNELS)
 
 
@@ -149,12 +151,16 @@ def tile_graphaugmentation_pb_t_kernel(tc, x, agg, g1w, g1b, g2w, g2b, out):
             image, columns = pixels_of(unit)
             slots = stream_slots[s][image][:, :, columns]
             grouped = work.tile(
-                [P, UNIT, PACK], BF16, tag="cat_grouped", bufs=3 * STREAMS, align_bytes=64
+                [P, UNIT, PACK],
+                BF16,
+                tag=("x_grouped", "agg_grouped")[s],
+                bufs=(2, 3)[s],
+                align_bytes=64,
             )
             regroup(
                 nc.scalar.copy, grouped[:, :SCALAR_PIXELS, :], slots[:, :, :SCALAR_PIXELS]
             )
-            if s == 0:
+            if s == 0 and unit >= FIRST_GPSIMD_UNIT:
                 nc.gpsimd.tensor_scalar(
                     out=grouped[:, SCALAR_PIXELS:, :],
                     in0=slots[:, :, SCALAR_PIXELS:].rearrange("p j w -> p w j"),

@@ -27,6 +27,16 @@ SCALAR_PIXELS = 192
 
 FIRST_GPSIMD_UNIT = 5
 
+LAST_PIXELS = 128
+LAST_PIECES = (
+    ("gpsimd", 0, 0, UNIT),
+    ("gpsimd", 1, 0, UNIT // 2),
+    ("vector", 1, UNIT // 2, UNIT),
+    ("vector", 2, 0, UNIT),
+    ("vector", 3, 0, UNIT - LAST_PIXELS),
+    ("vector", 3, UNIT - LAST_PIXELS, UNIT),
+)
+
 FLOPS = 2 * IMAGES * PIXELS * (CHANNELS * STREAMS * CHANNELS + CHANNELS * CHANNELS)
 
 
@@ -246,18 +256,21 @@ def tile_graphaugmentation_pb_t_kernel(tc, x, agg, g1w, g1b, g2w, g2b, out):
         def sigmoid_gate(unit):
             slots = work.tile([P, PACK, UNIT], F32, tag="gate_slots", bufs=4)
             for j in range(PACK):
-                nc.scalar.activation(
-                    out=slots[:, j, :],
-                    in_=gate_banks[unit, j][:],
-                    func=ACT.Sigmoid,
-                    bias=bias2[:, j : j + 1],
-                )
+                cuts = (0, UNIT - LAST_PIXELS, UNIT) if (unit, j) == (UNITS - 1, PACK - 1) else (0, UNIT)
+                for first, end in zip(cuts[:-1], cuts[1:]):
+                    nc.scalar.activation(
+                        out=slots[:, j, first:end],
+                        in_=gate_banks[unit, j][:, first:end],
+                        func=ACT.Sigmoid,
+                        bias=bias2[:, j : j + 1],
+                    )
             gate_slots[unit] = slots
 
         def agg_to_psum(unit):
             image, columns = pixels_of(unit)
             for pair in range(PACK // 2):
-                bank = vector_banks.tile([P, 2, UNIT], BF16, tag="bank")
+                banks = scalar_banks if unit == UNITS - 1 else vector_banks
+                bank = banks.tile([P, 2, UNIT], BF16, tag="bank")
                 for e in range(2):
                     nc.tensor.matmul(
                         out=bank[:, e, :],
@@ -286,6 +299,29 @@ def tile_graphaugmentation_pb_t_kernel(tc, x, agg, g1w, g1b, g2w, g2b, out):
                         out=out_view[image][:, done, columns], in_=result[:, done, :]
                     )
 
+        def last_products_and_stores(unit):
+            image, columns = pixels_of(unit)
+            result = gate_slots[unit]
+            for engine, j, first, end in LAST_PIECES:
+                piece = slice(first, end)
+                pixels = slice(columns.start + first, columns.start + end)
+                if engine == "gpsimd":
+                    nc.gpsimd.tensor_tensor(
+                        out=result[:, j, piece],
+                        in0=stream_slots[1][image][:, j, pixels],
+                        in1=result[:, j, piece],
+                        op=ALU.mult,
+                    )
+                    nc.scalar.dma_start(out=out_view[image][:, j, pixels], in_=result[:, j, piece])
+                else:
+                    nc.vector.tensor_tensor(
+                        out=result[:, j, piece],
+                        in0=agg_banks[unit, j // 2][:, j % 2, piece],
+                        in1=result[:, j, piece],
+                        op=ALU.mult,
+                    )
+                    nc.sync.dma_start(out=out_view[image][:, j, pixels], in_=result[:, j, piece])
+
         transpose_weight(w1_rows, STREAMS, w1_grouped)
         regroup_stream(0, 0)
         regroup_stream(0, 1)
@@ -305,7 +341,10 @@ def tile_graphaugmentation_pb_t_kernel(tc, x, agg, g1w, g1b, g2w, g2b, out):
             if 1 <= i <= UNITS:
                 second_matmul(i - 1)
             if i >= 2:
-                multiply_and_store(i - 2, slots_in_a_store=1 if i - 2 == UNITS - 1 else PACK)
+                if i - 2 == UNITS - 1:
+                    last_products_and_stores(i - 2)
+                else:
+                    multiply_and_store(i - 2, slots_in_a_store=2 if i - 2 >= UNITS - 3 else PACK)
             if 1 <= i <= UNITS:
                 agg_to_psum(i - 1)
             if i < UNITS:

@@ -79,7 +79,10 @@ def tile_graphaugmentation_pb_t_kernel(tc, x, agg, g1w, g1b, g2w, g2b, out):
                 )
 
         w1_rows = keep.tile([P, PACK * STREAMS * K_PASS], BF16)
-        nc.sync.dma_start(out=w1_rows[:], in_=g1w.rearrange("(m j) k -> m (j k)", j=PACK))
+        w1_row_slots = w1_rows[:].rearrange("m (j k) -> m j k", j=PACK)
+        g1w_row_slots = g1w.rearrange("(m j) k -> m j k", j=PACK)
+        for j in range(PACK):
+            nc.sync.dma_start(out=w1_row_slots[:, j, :], in_=g1w_row_slots[:, j, :])
         load_pixels(0, 0, UNIT)
         w2_rows = keep.tile([P, PACK * K_PASS], BF16)
         nc.sync.dma_start(out=w2_rows[:], in_=g2w.rearrange("(m j) k -> m (j k)", j=PACK))
@@ -95,10 +98,6 @@ def tile_graphaugmentation_pb_t_kernel(tc, x, agg, g1w, g1b, g2w, g2b, out):
         nc.scalar.dma_start(out=bias1_bf16[:], in_=g1b.rearrange("(m j) -> m j", j=PACK))
         bias2_bf16 = keep.tile([P, PACK], BF16)
         nc.scalar.dma_start(out=bias2_bf16[:], in_=g2b.rearrange("(m j) -> m j", j=PACK))
-        bias1 = keep.tile([P, PACK], F32)
-        nc.vector.tensor_copy(out=bias1[:], in_=bias1_bf16[:])
-        bias2 = keep.tile([P, PACK], F32)
-        nc.vector.tensor_copy(out=bias2[:], in_=bias2_bf16[:])
 
         identity_f32 = keep.tile([P, P], F32)
         make_identity(nc, identity_f32[:])
@@ -225,7 +224,7 @@ def tile_graphaugmentation_pb_t_kernel(tc, x, agg, g1w, g1b, g2w, g2b, out):
                     out=slots[:, j, :],
                     in_=hidden_banks[unit, j][:],
                     func=ACT.Relu,
-                    bias=bias1[:, j : j + 1],
+                    bias=bias1_bf16[:, j : j + 1],
                 )
             hidden_slots[unit] = slots
 
@@ -262,7 +261,7 @@ def tile_graphaugmentation_pb_t_kernel(tc, x, agg, g1w, g1b, g2w, g2b, out):
                         out=slots[:, j, first:end],
                         in_=gate_banks[unit, j][:, first:end],
                         func=ACT.Sigmoid,
-                        bias=bias2[:, j : j + 1],
+                        bias=bias2_bf16[:, j : j + 1],
                     )
             gate_slots[unit] = slots
 

@@ -26,6 +26,7 @@ UNITS = IMAGES * UNITS_PER_IMAGE
 SCALAR_PIXELS = 192
 
 FIRST_GPSIMD_UNIT = 5
+SCALAR_PIXELS_BESIDE_GPSIMD = (128, 232)
 
 LAST_PIXELS = 128
 LAST_PIECES = (
@@ -166,13 +167,16 @@ def tile_graphaugmentation_pb_t_kernel(tc, x, agg, g1w, g1b, g2w, g2b, out):
                 bufs=(2, 3)[s],
                 align_bytes=64,
             )
+            scalar_pixels = SCALAR_PIXELS
+            if unit >= FIRST_GPSIMD_UNIT:
+                scalar_pixels = SCALAR_PIXELS_BESIDE_GPSIMD[s]
             regroup(
-                nc.scalar.copy, grouped[:, :SCALAR_PIXELS, :], slots[:, :, :SCALAR_PIXELS]
+                nc.scalar.copy, grouped[:, :scalar_pixels, :], slots[:, :, :scalar_pixels]
             )
             if s == 0 and unit >= FIRST_GPSIMD_UNIT:
                 nc.gpsimd.tensor_scalar(
-                    out=grouped[:, SCALAR_PIXELS:, :],
-                    in0=slots[:, :, SCALAR_PIXELS:].rearrange("p j w -> p w j"),
+                    out=grouped[:, scalar_pixels:, :],
+                    in0=slots[:, :, scalar_pixels:].rearrange("p j w -> p w j"),
                     scalar1=1.0,
                     scalar2=0.0,
                     op0=ALU.mult,
@@ -181,8 +185,8 @@ def tile_graphaugmentation_pb_t_kernel(tc, x, agg, g1w, g1b, g2w, g2b, out):
             else:
                 regroup(
                     nc.vector.tensor_copy,
-                    grouped[:, SCALAR_PIXELS:, :],
-                    slots[:, :, SCALAR_PIXELS:],
+                    grouped[:, scalar_pixels:, :],
+                    slots[:, :, scalar_pixels:],
                 )
             cat_grouped[unit, s] = grouped
 

from contextlib import ExitStack

import concourse.mybir as mybir
from concourse.masks import make_identity

BF16 = mybir.dt.bfloat16
F32 = mybir.dt.float32
U32 = mybir.dt.uint32
U8 = mybir.dt.uint8
FP8X4 = mybir.dt.float8_e4m3fn_x4
ACT = mybir.ActivationFunctionType
ALU = mybir.AluOpType

P = 128
PACK = 4
K_PASS = P * PACK

IMAGES = 6
CHANNELS = 512
PIXELS = 1024
STREAMS = 2
UNIT = 512
UNITS_PER_IMAGE = PIXELS // UNIT
UNITS = IMAGES * UNITS_PER_IMAGE

SCALAR_PIXELS = 192

FIRST_GPSIMD_UNIT = 5
SCALAR_PIXELS_BESIDE_GPSIMD = (128, 232)

LAST_PIXELS = 128
LAST_PIECES = (
    ("gpsimd", 0, 0, UNIT),
    ("gpsimd", 1, 0, UNIT // 2),
    ("vector", 1, UNIT // 2, UNIT),
    ("vector", 2, 0, UNIT),
    ("vector", 3, 0, UNIT - LAST_PIXELS),
    ("vector", 3, UNIT - LAST_PIXELS, UNIT),
)

FLOPS = 2 * IMAGES * PIXELS * (CHANNELS * STREAMS * CHANNELS + CHANNELS * CHANNELS)


def regroup(copy, grouped, slots):
    copy(
        out=grouped.rearrange("p (c i) j -> p c j i", i=4),
        in_=slots.rearrange("p j (c i) -> p c j i", i=4),
    )


def tile_graphaugmentation_pb_t_kernel(tc, x, agg, g1w, g1b, g2w, g2b, out):
    nc = tc.nc
    stream_views = [
        x.rearrange("b (p j) h w -> b p j (h w)", j=PACK),
        agg.rearrange("b (p j) h w -> b p j (h w)", j=PACK),
    ]
    out_view = out.rearrange("b (p j) h w -> b p j (h w)", j=PACK)

    with ExitStack() as ctx:
        keep = ctx.enter_context(tc.tile_pool(name="keep", bufs=1))
        inputs = ctx.enter_context(tc.tile_pool(name="inputs", bufs=IMAGES))
        work = ctx.enter_context(tc.tile_pool(name="work", bufs=2))
        scalar_banks = ctx.enter_context(tc.psum_pool(name="scalar_banks", bufs=6))
        vector_banks = ctx.enter_context(tc.psum_pool(name="vector_banks", bufs=2))
        ctx.enter_context(tc.manual_schedule())

        stream_slots = [[], []]
        for b in range(IMAGES):
            x_image = inputs.tile([P, PACK, PIXELS], BF16, tag="x")
            stream_slots[0].append(x_image)
            agg_image = inputs.tile([P, PACK, PIXELS], BF16, tag="agg")
            stream_slots[1].append(agg_image)

        def load_pixels(image, first, count):
            columns = slice(first, first + count)
            for s in range(STREAMS):
                nc.sync.dma_start(
                    out=stream_slots[s][image][:, :, columns],
                    in_=stream_views[s][image][:, :, columns],
                )

        w1_rows = keep.tile([P, PACK * STREAMS * K_PASS], BF16)
        w1_row_slots = w1_rows[:].rearrange("m (j k) -> m j k", j=PACK)
        g1w_row_slots = g1w.rearrange("(m j) k -> m j k", j=PACK)
        for j in range(PACK):
            nc.sync.dma_start(out=w1_row_slots[:, j, :], in_=g1w_row_slots[:, j, :])
        load_pixels(0, 0, UNIT)
        w2_rows = keep.tile([P, PACK * K_PASS], BF16)
        nc.sync.dma_start(out=w2_rows[:], in_=g2w.rearrange("(m j) k -> m (j k)", j=PACK))
        load_pixels(0, UNIT, UNIT)
        for b in range(1, IMAGES):
            load_pixels(b, 0, PIXELS)

        table_warmer = keep.tile([P, 1], F32)
        nc.vector.memset(table_warmer[:], 0.0)
        nc.scalar.activation(out=table_warmer[:], in_=table_warmer[:], func=ACT.Sigmoid)

        bias1_bf16 = keep.tile([P, PACK], BF16)
        nc.scalar.dma_start(out=bias1_bf16[:], in_=g1b.rearrange("(m j) -> m j", j=PACK))
        bias2_bf16 = keep.tile([P, PACK], BF16)
        nc.scalar.dma_start(out=bias2_bf16[:], in_=g2b.rearrange("(m j) -> m j", j=PACK))

        identity_f32 = keep.tile([P, P], F32)
        make_identity(nc, identity_f32[:])
        identity_bf16 = keep.tile([P, P], BF16)
        make_identity(nc, identity_bf16[:])

        def transpose_weight(rows, passes, grouped):
            tiles = PACK * passes
            words = rows[:].bitcast(F32).rearrange("m (c p u) -> m c u p", c=tiles, u=2)
            grouped_words = grouped[:].bitcast(F32).rearrange(
                "p (c m u) -> p c m u", c=tiles, u=2
            )
            for pair in range(tiles // 2):
                if pair % 2 == 0:
                    bank = vector_banks.tile([P, UNIT], F32, tag="bank")
                    copy = nc.vector.tensor_copy
                else:
                    bank = scalar_banks.tile([P, UNIT], F32, tag="bank")
                    copy = nc.scalar.copy
                transposed = bank[:].rearrange("p (c u m) -> p c u m", c=2, u=2)
                for c in range(2):
                    for u in range(2):
                        nc.tensor.transpose(
                            transposed[:, c, u, :],
                            words[:, 2 * pair + c, u, :],
                            identity_f32[:],
                        )
                copy(
                    out=grouped_words[:, 2 * pair : 2 * pair + 2, :, :],
                    in_=transposed.rearrange("p c u m -> p c m u"),
                )

        def quantise_weight(grouped, codes, scales):
            nc.vector.quantize_mx(
                out=codes[:].bitcast(FP8X4), scales=scales[:], in_=grouped[:]
            )

        w1_grouped = keep.tile([P, PACK * STREAMS * P * PACK], BF16, align_bytes=64)
        w1_codes = keep.tile([P, PACK * STREAMS * P], U32, align_bytes=64)
        w1_scales = keep.tile([P, PACK * STREAMS * P], U8, align_bytes=64)
        w2_grouped = keep.tile([P, PACK * P * PACK], BF16, align_bytes=64)
        w2_codes = keep.tile([P, PACK * P], U32, align_bytes=64)
        w2_scales = keep.tile([P, PACK * P], U8, align_bytes=64)

        cat_grouped = {}
        cat_quantised = {}
        hidden_banks = {}
        hidden_slots = {}
        hidden_grouped = {}
        hidden_quantised = {}
        gate_banks = {}
        gate_slots = {}
        agg_banks = {}

        def pixels_of(unit):
            image, half = divmod(unit, UNITS_PER_IMAGE)
            return image, slice(half * UNIT, (half + 1) * UNIT)

        def regroup_stream(unit, s):
            image, columns = pixels_of(unit)
            slots = stream_slots[s][image][:, :, columns]
            grouped = work.tile(
                [P, UNIT, PACK],
                BF16,
                tag=("x_grouped", "agg_grouped")[s],
                bufs=(2, 3)[s],
                align_bytes=64,
            )
            scalar_pixels = SCALAR_PIXELS
            if unit >= FIRST_GPSIMD_UNIT:
                scalar_pixels = SCALAR_PIXELS_BESIDE_GPSIMD[s]
            regroup(
                nc.scalar.copy, grouped[:, :scalar_pixels, :], slots[:, :, :scalar_pixels]
            )
            if s == 0 and unit >= FIRST_GPSIMD_UNIT:
                nc.gpsimd.tensor_scalar(
                    out=grouped[:, scalar_pixels:, :],
                    in0=slots[:, :, scalar_pixels:].rearrange("p j w -> p w j"),
                    scalar1=1.0,
                    scalar2=0.0,
                    op0=ALU.mult,
                    op1=ALU.add,
                )
            else:
                regroup(
                    nc.vector.tensor_copy,
                    grouped[:, scalar_pixels:, :],
                    slots[:, :, scalar_pixels:],
                )
            cat_grouped[unit, s] = grouped

        def quantise(grouped, tag, bufs):
            codes = work.tile([P, UNIT], U32, tag=tag + "_codes", bufs=bufs, align_bytes=64)
            scales = work.tile([P, UNIT], U8, tag=tag + "_scales", bufs=bufs, align_bytes=64)
            nc.vector.quantize_mx(
                out=codes[:].bitcast(FP8X4),
                scales=scales[:],
                in_=grouped[:].rearrange("p w j -> p (w j)"),
            )
            return codes, scales

        def quantise_cat(unit):
            for s in range(STREAMS):
                cat_quantised[unit, s] = quantise(cat_grouped[unit, s], "cat", 2 * STREAMS)

        def first_matmul(unit):
            for j in range(PACK):
                bank = scalar_banks.tile([P, UNIT], F32, tag="bank")
                for s in range(STREAMS):
                    columns = slice((j * STREAMS + s) * P, (j * STREAMS + s + 1) * P)
                    codes, scales = cat_quantised[unit, s]
                    nc.tensor.matmul_mx(
                        out=bank[:],
                        lhsT=w1_codes[:, columns].bitcast(FP8X4),
                        lhsT_scale=w1_scales[:, columns],
                        rhs=codes[:].bitcast(FP8X4),
                        rhs_scale=scales[:],
                        start=(s == 0),
                        stop=(s == STREAMS - 1),
                    )
                hidden_banks[unit, j] = bank

        def relu_hidden(unit):
            slots = work.tile([P, PACK, UNIT], BF16, tag="hidden_slots")
            for j in range(PACK):
                nc.scalar.activation(
                    out=slots[:, j, :],
                    in_=hidden_banks[unit, j][:],
                    func=ACT.Relu,
                    bias=bias1_bf16[:, j : j + 1],
                )
            hidden_slots[unit] = slots

        def regroup_hidden(unit):
            grouped = work.tile([P, UNIT, PACK], BF16, tag="hidden_grouped", align_bytes=64)
            regroup(nc.vector.tensor_copy, grouped[:], hidden_slots[unit][:])
            hidden_grouped[unit] = grouped

        def quantise_hidden(unit):
            hidden_quantised[unit] = quantise(hidden_grouped[unit], "hidden", 2)

        def second_matmul(unit):
            codes, scales = hidden_quantised[unit]
            for j in range(PACK):
                bank = scalar_banks.tile([P, UNIT], F32, tag="bank")
                columns = slice(j * P, (j + 1) * P)
                nc.tensor.matmul_mx(
                    out=bank[:],
                    lhsT=w2_codes[:, columns].bitcast(FP8X4),
                    lhsT_scale=w2_scales[:, columns],
                    rhs=codes[:].bitcast(FP8X4),
                    rhs_scale=scales[:],
                    start=True,
                    stop=True,
                )
                gate_banks[unit, j] = bank

        def sigmoid_gate(unit):
            slots = work.tile([P, PACK, UNIT], F32, tag="gate_slots", bufs=4)
            for j in range(PACK):
                cuts = (0, UNIT - LAST_PIXELS, UNIT) if (unit, j) == (UNITS - 1, PACK - 1) else (0, UNIT)
                for first, end in zip(cuts[:-1], cuts[1:]):
                    nc.scalar.activation(
                        out=slots[:, j, first:end],
                        in_=gate_banks[unit, j][:, first:end],
                        func=ACT.Sigmoid,
                        bias=bias2_bf16[:, j : j + 1],
                    )
            gate_slots[unit] = slots

        def agg_to_psum(unit):
            image, columns = pixels_of(unit)
            for pair in range(PACK // 2):
                banks = scalar_banks if unit == UNITS - 1 else vector_banks
                bank = banks.tile([P, 2, UNIT], BF16, tag="bank")
                for e in range(2):
                    nc.tensor.matmul(
                        out=bank[:, e, :],
                        lhsT=identity_bf16[:],
                        rhs=stream_slots[1][image][:, 2 * pair + e, columns],
                        start=True,
                        stop=True,
                    )
                agg_banks[unit, pair] = bank

        def multiply_and_store(unit, slots_in_a_store):
            image, columns = pixels_of(unit)
            result = gate_slots[unit]
            slots_in_a_product = min(2, slots_in_a_store)
            for j in range(0, PACK, slots_in_a_product):
                slots = slice(j, j + slots_in_a_product)
                nc.vector.tensor_tensor(
                    out=result[:, slots, :],
                    in0=agg_banks[unit, j // 2][:, j % 2 : j % 2 + slots_in_a_product, :],
                    in1=result[:, slots, :],
                    op=ALU.mult,
                )
                if (j + slots_in_a_product) % slots_in_a_store == 0:
                    done = slice(j + slots_in_a_product - slots_in_a_store, j + slots_in_a_product)
                    nc.sync.dma_start(
                        out=out_view[image][:, done, columns], in_=result[:, done, :]
                    )

        def last_products_and_stores(unit):
            image, columns = pixels_of(unit)
            result = gate_slots[unit]
            for engine, j, first, end in LAST_PIECES:
                piece = slice(first, end)
                pixels = slice(columns.start + first, columns.start + end)
                if engine == "gpsimd":
                    nc.gpsimd.tensor_tensor(
                        out=result[:, j, piece],
                        in0=stream_slots[1][image][:, j, pixels],
                        in1=result[:, j, piece],
                        op=ALU.mult,
                    )
                    nc.scalar.dma_start(out=out_view[image][:, j, pixels], in_=result[:, j, piece])
                else:
                    nc.vector.tensor_tensor(
                        out=result[:, j, piece],
                        in0=agg_banks[unit, j // 2][:, j % 2, piece],
                        in1=result[:, j, piece],
                        op=ALU.mult,
                    )
                    nc.sync.dma_start(out=out_view[image][:, j, pixels], in_=result[:, j, piece])

        transpose_weight(w1_rows, STREAMS, w1_grouped)
        regroup_stream(0, 0)
        regroup_stream(0, 1)
        transpose_weight(w2_rows, 1, w2_grouped)
        quantise_weight(w1_grouped, w1_codes, w1_scales)
        quantise_cat(0)
        first_matmul(0)
        regroup_stream(1, 0)
        regroup_stream(1, 1)
        quantise_weight(w2_grouped, w2_codes, w2_scales)

        for i in range(UNITS + 2):
            if i + 1 < UNITS:
                quantise_cat(i + 1)
            if i < UNITS:
                relu_hidden(i)
            if 1 <= i <= UNITS:
                second_matmul(i - 1)
            if i >= 2:
                if i - 2 == UNITS - 1:
                    last_products_and_stores(i - 2)
                else:
                    multiply_and_store(i - 2, slots_in_a_store=2 if i - 2 >= UNITS - 3 else PACK)
            if 1 <= i <= UNITS:
                agg_to_psum(i - 1)
            if i < UNITS:
                regroup_hidden(i)
            if i + 2 < UNITS:
                regroup_stream(i + 2, 0)
            if 1 <= i <= UNITS:
                sigmoid_gate(i - 1)
            if i + 1 < UNITS:
                first_matmul(i + 1)
            if i + 2 < UNITS:
                regroup_stream(i + 2, 1)
            if i < UNITS:
                quantise_hidden(i)
